import numpy as np
import ml_dtypes


def mxq(x, axis, fmt="e4m3"):
    dtype, down = {"e4m3": (ml_dtypes.float8_e4m3fn, 7), "e5m2": (ml_dtypes.float8_e5m2, 14)}[fmt]
    v = np.moveaxis(np.asarray(x, np.float32).astype(ml_dtypes.bfloat16).astype(np.float64), axis, -1)
    blocks = v.reshape(v.shape[:-1] + (-1, 32))
    amax = np.abs(blocks).max(-1, keepdims=True)
    byte = np.maximum(np.where(amax > 0, np.frexp(amax)[1] - 1 + 127, 0) - down, 1)
    scale = np.exp2(byte - 127.0)
    codes = (blocks / scale).astype(np.float32).astype(dtype).astype(np.float64)
    return np.moveaxis((codes * scale).reshape(v.shape), -1, axis)


WIDE = False


def mx_kscale(k):
    if not WIDE:
        return np.ones(k)
    levels = np.array([10, -10, 5, -5, 0])
    if k % 512:
        return np.exp2(np.random.permutation(np.resize(levels, k // 32))).repeat(32)
    a = np.empty((k // 512, 16))
    for p in range(k // 512):
        a[p, :8] = np.random.permutation(np.resize(levels, 8))
        for g in range(8):
            far = levels[np.abs(levels - a[p, g]) >= 10]
            a[p, g + 8] = far[np.random.randint(len(far))]
    return np.exp2(a.ravel()).repeat(32)


BF16 = ml_dtypes.bfloat16


def bf(x):
    return np.asarray(x, np.float32).astype(BF16)


def f64(x):
    return np.asarray(x).astype(np.float64)


B, T, C, E, DV, R, G, BLK = 1, 1024, 1024, 1024, 1024, 16, 16, 512
BASE = 1e4


def rope(x):
    inv_freq = 1.0 / (BASE ** (f64(np.arange(0, R, 2)) / R))
    ang = f64(np.arange(T))[:, None] * inv_freq[None, :]
    ang = np.repeat(ang, 2, axis=-1)
    cos, sin = np.cos(ang), np.sin(ang)
    xl, xr = x[..., :R], x[..., R:]
    p = xl.reshape(xl.shape[:-1] + (R // 2, 2))
    rot = np.stack((-p[..., 1], p[..., 0]), axis=-1).reshape(xl.shape)
    return np.concatenate([xl * cos + rot * sin, xr], axis=-1)


def draw0():
    s = mx_kscale(C)
    return {"Q_in": bf(np.random.standard_normal((B, T, C)) * s),
            "W_Q": bf(np.random.standard_normal((C, E)) * 0.25 / np.sqrt(C) / s[:, None]),
            "W_K": bf(np.random.standard_normal((C, E)) * 0.25 / np.sqrt(C) / s[:, None])}


def core(Q_in, W_Q, W_K):
    xq = mxq(f64(Q_in), 2, "e4m3")
    q = rope(xq @ mxq(f64(W_Q), 0, "e4m3"))
    k = rope(xq @ mxq(f64(W_K), 0, "e4m3"))
    return q, k


def e4m3fn_bytes(y):
    return np.clip(np.asarray(y, np.float64), -448.0, 448.0).astype(np.float32).astype(ml_dtypes.float8_e4m3fn).view(np.uint8)


def e4m3fn_values(b):
    return np.asarray(b, np.uint8).view(ml_dtypes.float8_e4m3fn).astype(np.float64)


def setup_inputs():
    d = draw0()
    x0 = np.asarray(d['W_Q']).astype(np.float64)
    s = (np.max(np.abs(x0), axis=(1,), keepdims=True) / 448.0).astype(np.float32)
    out = {}
    for k, v in d.items():
        if k == 'W_Q':
            out['W_Q_bytes'] = e4m3fn_bytes(x0 / s.astype(np.float64))
            out['W_Q_scale'] = s
        else:
            out[k] = v
    return out


def reference(Q_in, W_Q_bytes, W_Q_scale, W_K):
    return core(Q_in, e4m3fn_values(W_Q_bytes) * W_Q_scale.astype(np.float64), W_K)

@@ -1,0 +1,255 @@
+from contextlib import ExitStack
+import math
+
+import concourse.mybir as mybir
+from concourse.masks import make_identity
+
+FLOPS = 2 * 1024 * 1024 * 2048
+
+F32 = mybir.dt.float32
+BF16 = mybir.dt.bfloat16
+U32 = mybir.dt.uint32
+U8 = mybir.dt.uint8
+I32 = mybir.dt.int32
+FP8 = mybir.dt.float8_e4m3fn
+FP8X4 = mybir.dt.float8_e4m3fn_x4
+ALU = mybir.AluOpType
+ACT = mybir.ActivationFunctionType
+
+P = 128
+NT = 8
+NG = 2
+NW = 512
+R = 16
+NJ = R // 2
+TWO_PI_HI = 6.28125
+TWO_PI_LO = 2.0 * math.pi - 6.28125
+
+Q1, K1, K0, Q0 = ("q", 1), ("k", 1), ("k", 0), ("q", 0)
+V_HEAD = ((0, 1, 0), (0, 1, 1), (0, 1, 2), (1, 1, 0), (1, 1, 1), (1, 1, 2))
+S_HEAD = ((0, 1, 3), (0, 0, 0), (1, 1, 3), (0, 0, 1))
+V_MID = ((0, 0, 2), (0, 0, 3), (1, 0, 0), (1, 0, 1), (1, 0, 2), (1, 0, 3))
+V_LAST = (1, 5)
+WARM_START = 8
+WARM_PLANES = ((0, 1, 0), (0, 1, 2), (1, 1, 0), (1, 1, 1))
+
+
+def tile_wqkv_pa_kernel(tc, Q_in, W_Q_bytes, W_Q_scale, W_K, out_0, out_1):
+    nc = tc.nc
+    with ExitStack() as ctx:
+        keep = ctx.enter_context(tc.tile_pool(name="keep", bufs=1))
+        psum_a = ctx.enter_context(tc.psum_pool(name="psum_a", bufs=6))
+        ctx.enter_context(tc.manual_schedule())
+
+        x_view = Q_in.rearrange("o (p i) k -> p (o i) k", i=NT)
+        wq_view = W_Q_bytes.rearrange("(g p t) n -> g p t n", p=P, t=4)
+        wk_view = W_K.rearrange("(g p t) n -> g p t n", p=P, t=4)
+        out_views = {
+            "q": out_0.rearrange("o (p i) n -> p (o i) n", i=NT),
+            "k": out_1.rearrange("o (p i) n -> p (o i) n", i=NT),
+        }
+
+        warm = keep.tile([P, NW], BF16, name="warm")
+        nc.vector.memset(warm[:], 0.0)
+        idle_bank = psum_a.tile([P, NW], F32, name="acc_a")
+
+        def keep_warm(rhs):
+            nc.tensor.matmul(out=idle_bank[:], lhsT=warm[:, 0:P], rhs=rhs, start=True, stop=True)
+
+        for n in range(WARM_START):
+            keep_warm(warm[:])
+
+        sc = keep.tile([P, NG, 4], F32, name="sc")
+        nc.scalar.dma_start(out=sc[:], in_=W_Q_scale.rearrange("(g p t) o -> p g (t o)", p=P, t=4))
+        wq_b = [keep.tile([P, 4, 1024], U8, name="wq_b%d" % g) for g in range(NG)]
+        x_raw = [keep.tile([P, 2, 1024], BF16, name="x_raw%d" % j) for j in range(NT // 2)]
+        wk_raw = [keep.tile([P, 4, 1024], BF16, name="wk_raw%d" % g) for g in range(NG)]
+        for g in range(NG):
+            nc.sync.dma_start(out=wq_b[g][:], in_=wq_view[g])
+        for j in range(NT // 2):
+            nc.sync.dma_start(out=x_raw[j][:], in_=x_view[:, 2 * j:2 * j + 2, :])
+        for g in range(NG):
+            nc.sync.dma_start(out=wk_raw[g][:], in_=wk_view[g])
+
+        pos_i = keep.tile([P, NT], I32, name="pos_i")
+        nc.gpsimd.iota(pos_i[:], pattern=[[1, NT]], base=0, channel_multiplier=NT)
+        ident = keep.tile([P, P], F32, name="ident")
+        make_identity(nc, ident[:])
+
+        def table_tile(name, dtype=F32):
+            return [keep.tile([P, NT, NJ], dtype, name="%s%d" % (name, s)) for s in range(2)]
+
+        z0 = table_tile("z0")
+        nc.vector.tensor_copy(out=z0[1][:, :, 0], in_=pos_i[:])
+        for n in (1, 2, 4):
+            nc.vector.tensor_scalar(out=z0[1][:, :, n:2 * n], in0=z0[1][:, :, 0:n], scalar1=10000.0 ** (-n / float(NJ)),
+                                    scalar2=None, op0=ALU.mult)
+        nc.vector.tensor_scalar(out=z0[0][:], in0=z0[1][:], scalar1=-0.5 * math.pi, scalar2=None, op0=ALU.add)
+        turns = table_tile("turns", I32)
+        z1, z2, y1, y1m, y2, arg = [table_tile(n) for n in ("z1", "z2", "y1", "y1m", "y2", "arg")]
+        for s in (1, 0):
+            nc.vector.tensor_scalar(out=turns[s][:], in0=z0[s][:], scalar1=1.0 / (2.0 * math.pi), scalar2=None, op0=ALU.mult)
+        for s in (1, 0):
+            nc.vector.scalar_tensor_tensor(out=z1[s][:], in0=turns[s][:], scalar=-TWO_PI_HI, in1=z0[s][:], op0=ALU.mult, op1=ALU.add)
+        for s in (1, 0):
+            nc.vector.scalar_tensor_tensor(out=z2[s][:], in0=turns[s][:], scalar=-TWO_PI_LO, in1=z1[s][:], op0=ALU.mult, op1=ALU.add)
+        for s in (1, 0):
+            nc.vector.scalar_tensor_tensor(out=y1[s][:], in0=z2[s][:], scalar=-1.0, in1=z2[s][:], op0=ALU.mult, op1=ALU.max)
+        for s in (1, 0):
+            nc.vector.tensor_scalar(out=y1m[s][:], in0=y1[s][:], scalar1=-math.pi, scalar2=None, op0=ALU.add)
+        for s in (1, 0):
+            nc.vector.scalar_tensor_tensor(out=y2[s][:], in0=y1m[s][:], scalar=-1.0, in1=y1m[s][:], op0=ALU.mult, op1=ALU.max)
+        for s in (1, 0):
+            nc.vector.tensor_scalar(out=arg[s][:], in0=y2[s][:], scalar1=-0.5 * math.pi, scalar2=None, op0=ALU.add)
+        cos_t = keep.tile([P, NT, R], F32, name="cos_t")
+        sin_t = keep.tile([P, NT, R], F32, name="sin_t")
+        nc.scalar.activation(out=cos_t[:, :, 0:R:2], in_=arg[1][:], func=ACT.Sin)
+        nc.scalar.activation(out=cos_t[:, :, 1:R:2], in_=arg[1][:], func=ACT.Sin)
+        nc.scalar.activation(out=sin_t[:, :, 0:R:2], in_=arg[0][:], func=ACT.Sin, scale=-1.0)
+        nc.scalar.activation(out=sin_t[:, :, 1:R:2], in_=arg[0][:], func=ACT.Sin)
+
+        x_grouped = [keep.tile([P, 2048], BF16, name="x_grouped%d" % j, align_bytes=64) for j in range(NT // 2)]
+        x_codes = [keep.tile([P, 512], U32, name="x_codes%d" % j, align_bytes=64) for j in range(NT // 2)]
+        x_scales = [keep.tile([P, 512], U8, name="x_scales%d" % j, align_bytes=64) for j in range(NT // 2)]
+
+        def turn_x(pool, i):
+            j, ii = divmod(i, 2)
+            grouped_words = x_grouped[j][:].bitcast(F32).rearrange("p (i g r u) -> p i g r u", i=2, g=NG, r=P, u=2)
+            words = x_raw[j][:, ii, :].bitcast(F32)
+            xt = pool.tile([P, NG, 2, P], F32, name="xt")
+            keep_warm(x_raw[j][:, ii, 0:NW])
+            for g in range(NG):
+                for u in range(2):
+                    nc.tensor.transpose(xt[:, g, u, :], words[:, 256 * g + u:256 * (g + 1):2], ident[:])
+            nc.scalar.copy(out=grouped_words[:, ii], in_=xt[:].rearrange("p g u r -> p g r u"))
+
+        def quantize_x(j):
+            nc.vector.quantize_mx(out=x_codes[j][:].bitcast(FP8X4), scales=x_scales[j][:], in_=x_grouped[j][:])
+
+        units = (Q1, K1, K0, Q0)
+        wq_w = [keep.tile([P, 4, 1024], BF16, name="wq_w%d" % g) for g in range(NG)]
+        w_grouped = {u: [keep.tile([P, NW, 4], BF16, name="w_grouped_%s%d_%d" % (u[0], u[1], g), align_bytes=64) for g in range(NG)] for u in units}
+        w_codes = {u: [keep.tile([P, NW], U32, name="w_codes_%s%d_%d" % (u[0], u[1], g), align_bytes=64) for g in range(NG)] for u in units}
+        w_scales = {u: [keep.tile([P, NW], U8, name="w_scales_%s%d_%d" % (u[0], u[1], g), align_bytes=64) for g in range(NG)] for u in units}
+        stage = {u: keep.tile([P, NT, NW], F32, name="stage_%s%d" % u) for u in units}
+
+        def widen(plane, on_scalar):
+            g, h, t = plane
+            cols = slice(h * NW, (h + 1) * NW)
+            src = wq_b[g][:, t, cols].bitcast(FP8)
+            if on_scalar:
+                nc.scalar.activation(out=wq_w[g][:, t, cols], in_=src, func=ACT.Copy, scale=sc[:, g, t:t + 1])
+            else:
+                nc.vector.tensor_scalar(out=wq_w[g][:, t, cols], in0=src, scalar1=sc[:, g, t:t + 1], scalar2=None, op0=ALU.mult)
+            if plane in WARM_PLANES:
+                keep_warm(wq_w[g][:, t, cols])
+
+        def interleave(u, g):
+            kind, h = u
+            src = wq_w[g] if kind == "q" else wk_raw[g]
+            nc.vector.tensor_copy(out=w_grouped[u][g][:].rearrange("p (c i) t -> p c t i", i=4),
+                                  in_=src[:, :, h * NW:(h + 1) * NW].rearrange("p t (c i) -> p c t i", i=4))
+
+        def quantize(u, g):
+            nc.vector.quantize_mx(out=w_codes[u][g][:].bitcast(FP8X4), scales=w_scales[u][g][:],
+                                  in_=w_grouped[u][g][:].rearrange("p c t -> p (c t)"))
+
+        def prep_w(u):
+            interleave(u, 0)
+            interleave(u, 1)
+            quantize(u, 0)
+            quantize(u, 1)
+
+        def rope_products(u, i0, i1):
+            x = stage[u]
+            t1 = keep.tile([P, i1 - i0, R], F32, name="t1_%s_%d" % (u[0], i0))
+            t2 = keep.tile([P, i1 - i0, R], F32, name="t2_%s_%d" % (u[0], i0))
+            nc.vector.tensor_tensor(out=t1[:], in0=x[:, i0:i1, 0:R], in1=cos_t[:, i0:i1, :], op=ALU.mult)
+            nc.vector.tensor_tensor(out=t2[:, :, 0:R:2], in0=x[:, i0:i1, 1:R:2], in1=sin_t[:, i0:i1, 0:R:2], op=ALU.mult)
+            nc.vector.tensor_tensor(out=t2[:, :, 1:R:2], in0=x[:, i0:i1, 0:R:2], in1=sin_t[:, i0:i1, 1:R:2], op=ALU.mult)
+            return t1, t2
+
+        def rope_sum(u, i0, i1, parts):
+            nc.vector.tensor_tensor(out=stage[u][:, i0:i1, 0:R], in0=parts[0][:], in1=parts[1][:], op=ALU.add)
+
+        def store(u, i0, i1):
+            kind, h = u
+            nc.sync.dma_start(out=out_views[kind][:, i0:i1, h * NW:(h + 1) * NW], in_=stage[u][:, i0:i1, :])
+
+        def one_pass(u, i, g, acc):
+            j, ii = divmod(i, 2)
+            cols = slice((ii * NG + g) * P, (ii * NG + g + 1) * P)
+            nc.tensor.matmul_mx(out=acc[:], lhsT=x_codes[j][:, cols].bitcast(FP8X4), lhsT_scale=x_scales[j][:, cols],
+                                rhs=w_codes[u][g][:].bitcast(FP8X4), rhs_scale=w_scales[u][g][:],
+                                start=(g == 0), stop=(g == NG - 1))
+
+        def empty(u, i, acc, on_vector):
+            if on_vector:
+                nc.vector.tensor_copy(out=stage[u][:, i, :], in_=acc[:])
+            else:
+                nc.scalar.copy(out=stage[u][:, i, :], in_=acc[:])
+
+        for plane in V_HEAD:
+            widen(plane, False)
+        for plane in S_HEAD:
+            widen(plane, True)
+        interleave(Q1, 0)
+        interleave(Q1, 1)
+        with tc.psum_pool(name="psum_x", bufs=2) as psum_x:
+            turn_x(psum_x, 0)
+            turn_x(psum_x, 1)
+            quantize_x(0)
+            quantize(Q1, 0)
+            quantize(Q1, 1)
+            for j in range(1, NT // 2):
+                turn_x(psum_x, 2 * j)
+                turn_x(psum_x, 2 * j + 1)
+                if j == NT // 2 - 1:
+                    interleave(K1, 0)
+                quantize_x(j)
+        psum_b = ctx.enter_context(tc.psum_pool(name="psum_b", bufs=2))
+
+        def bank(i):
+            if i < 6:
+                acc = psum_a.tile([P, NW], F32, name="acc_a")
+            else:
+                acc = psum_b.tile([P, NW], F32, name="acc_b")
+            return acc
+
+        def tiles(u, i0, i1):
+            for i in range(i0, i1):
+                acc = bank(i)
+                one_pass(u, i, 0, acc)
+                one_pass(u, i, 1, acc)
+                empty(u, i, acc, False)
+
+        interleave(K1, 1)
+        quantize(K1, 0)
+        quantize(K1, 1)
+        for i in range(0, NT, 2):
+            tiles(Q1, i, i + 2)
+            store(Q1, i, i + 2)
+        prep_w(K0)
+        for i in range(0, NT, 2):
+            tiles(K1, i, i + 2)
+            store(K1, i, i + 2)
+        for plane in V_MID:
+            widen(plane, False)
+        for g in range(NG):
+            i0 = 4 * g
+            interleave(Q0, g)
+            tiles(K0, i0, i0 + 4)
+            parts = rope_products(K0, i0, i0 + 4)
+            quantize(Q0, g)
+            rope_sum(K0, i0, i0 + 4, parts)
+            store(K0, i0, i0 + 4)
+        banks = [bank(i) for i in range(NT)]
+        for i in range(NT):
+            one_pass(Q0, i, 0, banks[i])
+        for i in range(NT):
+            one_pass(Q0, i, 1, banks[i])
+            empty(Q0, i, banks[i], i in V_LAST)
+            if i % 2 == 1:
+                parts = rope_products(Q0, i - 1, i + 1)
+                rope_sum(Q0, i - 1, i + 1, parts)
+                store(Q0, i - 1, i + 1)

@@ -26,12 +26,9 @@ TWO_PI_HI = 6.28125
 TWO_PI_LO = 2.0 * math.pi - 6.28125
 
 Q1, K1, K0, Q0 = ("q", 1), ("k", 1), ("k", 0), ("q", 0)
-V_HEAD = ((0, 1, 0), (0, 1, 1), (0, 1, 2), (1, 1, 0), (1, 1, 1), (1, 1, 2))
-S_HEAD = ((0, 1, 3), (0, 0, 0), (1, 1, 3), (0, 0, 1))
 V_MID = ((0, 0, 2), (0, 0, 3), (1, 0, 0), (1, 0, 1), (1, 0, 2), (1, 0, 3))
 V_LAST = (1, 5)
-WARM_START = 8
-WARM_PLANES = ((0, 1, 0), (0, 1, 2), (1, 1, 0), (1, 1, 1))
+WARM_START = 5
 
 
 def tile_wqkv_pa_kernel(tc, Q_in, W_Q_bytes, W_Q_scale, W_K, out_0, out_1):
@@ -49,8 +46,10 @@ def tile_wqkv_pa_kernel(tc, Q_in, W_Q_bytes, W_Q_scale, W_K, out_0, out_1):
             "k": out_1.rearrange("o (p i) n -> p (o i) n", i=NT),
         }
 
+        pos_i = keep.tile([P, NT], I32, name="pos_i")
+        nc.gpsimd.iota(pos_i[:], pattern=[[1, NT]], base=0, channel_multiplier=NT)
         warm = keep.tile([P, NW], BF16, name="warm")
-        nc.vector.memset(warm[:], 0.0)
+        nc.gpsimd.memset(warm[:], 0.0)
         idle_bank = psum_a.tile([P, NW], F32, name="acc_a")
 
         def keep_warm(rhs):
@@ -61,18 +60,27 @@ def tile_wqkv_pa_kernel(tc, Q_in, W_Q_bytes, W_Q_scale, W_K, out_0, out_1):
 
         sc = keep.tile([P, NG, 4], F32, name="sc")
         nc.scalar.dma_start(out=sc[:], in_=W_Q_scale.rearrange("(g p t) o -> p g (t o)", p=P, t=4))
+        preload = keep.tile([P, 1], F32, name="preload")
+        nc.scalar.activation(out=preload[:], in_=warm[:, 0:1], func=ACT.Sin)
         wq_b = [keep.tile([P, 4, 1024], U8, name="wq_b%d" % g) for g in range(NG)]
         x_raw = [keep.tile([P, 2, 1024], BF16, name="x_raw%d" % j) for j in range(NT // 2)]
         wk_raw = [keep.tile([P, 4, 1024], BF16, name="wk_raw%d" % g) for g in range(NG)]
-        for g in range(NG):
+
+        def load_wq(g):
             nc.sync.dma_start(out=wq_b[g][:], in_=wq_view[g])
-        for j in range(NT // 2):
+
+        def load_x(j):
             nc.sync.dma_start(out=x_raw[j][:], in_=x_view[:, 2 * j:2 * j + 2, :])
+
+        load_wq(0)
+        load_x(0)
+        load_x(1)
+        load_wq(1)
+        load_x(2)
+        load_x(3)
         for g in range(NG):
             nc.sync.dma_start(out=wk_raw[g][:], in_=wk_view[g])
 
-        pos_i = keep.tile([P, NT], I32, name="pos_i")
-        nc.gpsimd.iota(pos_i[:], pattern=[[1, NT]], base=0, channel_multiplier=NT)
         ident = keep.tile([P, P], F32, name="ident")
         make_identity(nc, ident[:])
 
@@ -86,27 +94,27 @@ def tile_wqkv_pa_kernel(tc, Q_in, W_Q_bytes, W_Q_scale, W_K, out_0, out_1):
                                     scalar2=None, op0=ALU.mult)
         nc.vector.tensor_scalar(out=z0[0][:], in0=z0[1][:], scalar1=-0.5 * math.pi, scalar2=None, op0=ALU.add)
         turns = table_tile("turns", I32)
-        z1, z2, y1, y1m, y2, arg = [table_tile(n) for n in ("z1", "z2", "y1", "y1m", "y2", "arg")]
+        z1, z2, y1, y2 = [table_tile(n) for n in ("z1", "z2", "y1", "y2")]
         for s in (1, 0):
             nc.vector.tensor_scalar(out=turns[s][:], in0=z0[s][:], scalar1=1.0 / (2.0 * math.pi), scalar2=None, op0=ALU.mult)
         for s in (1, 0):
             nc.vector.scalar_tensor_tensor(out=z1[s][:], in0=turns[s][:], scalar=-TWO_PI_HI, in1=z0[s][:], op0=ALU.mult, op1=ALU.add)
         for s in (1, 0):
             nc.vector.scalar_tensor_tensor(out=z2[s][:], in0=turns[s][:], scalar=-TWO_PI_LO, in1=z1[s][:], op0=ALU.mult, op1=ALU.add)
-        for s in (1, 0):
-            nc.vector.scalar_tensor_tensor(out=y1[s][:], in0=z2[s][:], scalar=-1.0, in1=z2[s][:], op0=ALU.mult, op1=ALU.max)
-        for s in (1, 0):
-            nc.vector.tensor_scalar(out=y1m[s][:], in0=y1[s][:], scalar1=-math.pi, scalar2=None, op0=ALU.add)
-        for s in (1, 0):
-            nc.vector.scalar_tensor_tensor(out=y2[s][:], in0=y1m[s][:], scalar=-1.0, in1=y1m[s][:], op0=ALU.mult, op1=ALU.max)
-        for s in (1, 0):
-            nc.vector.tensor_scalar(out=arg[s][:], in0=y2[s][:], scalar1=-0.5 * math.pi, scalar2=None, op0=ALU.add)
         cos_t = keep.tile([P, NT, R], F32, name="cos_t")
         sin_t = keep.tile([P, NT, R], F32, name="sin_t")
-        nc.scalar.activation(out=cos_t[:, :, 0:R:2], in_=arg[1][:], func=ACT.Sin)
-        nc.scalar.activation(out=cos_t[:, :, 1:R:2], in_=arg[1][:], func=ACT.Sin)
-        nc.scalar.activation(out=sin_t[:, :, 0:R:2], in_=arg[0][:], func=ACT.Sin, scale=-1.0)
-        nc.scalar.activation(out=sin_t[:, :, 1:R:2], in_=arg[0][:], func=ACT.Sin)
+
+        def table_step(n):
+            if n < 2:
+                nc.scalar.activation(out=y1[1 - n][:], in_=z2[1 - n][:], func=ACT.Abs)
+            elif n < 4:
+                nc.scalar.activation(out=y2[3 - n][:], in_=y1[3 - n][:], func=ACT.Abs, bias=-math.pi)
+            elif n < 6:
+                nc.scalar.activation(out=cos_t[:, :, n - 4:R:2], in_=y2[1][:], func=ACT.Sin, bias=-0.5 * math.pi)
+            elif n == 6:
+                nc.scalar.activation(out=sin_t[:, :, 0:R:2], in_=y2[0][:], func=ACT.Sin, scale=-1.0, bias=0.5 * math.pi)
+            else:
+                nc.scalar.activation(out=sin_t[:, :, 1:R:2], in_=y2[0][:], func=ACT.Sin, bias=-0.5 * math.pi)
 
         x_grouped = [keep.tile([P, 2048], BF16, name="x_grouped%d" % j, align_bytes=64) for j in range(NT // 2)]
         x_codes = [keep.tile([P, 512], U32, name="x_codes%d" % j, align_bytes=64) for j in range(NT // 2)]
@@ -122,6 +130,7 @@ def tile_wqkv_pa_kernel(tc, Q_in, W_Q_bytes, W_Q_scale, W_K, out_0, out_1):
                 for u in range(2):
                     nc.tensor.transpose(xt[:, g, u, :], words[:, 256 * g + u:256 * (g + 1):2], ident[:])
             nc.scalar.copy(out=grouped_words[:, ii], in_=xt[:].rearrange("p g u r -> p g r u"))
+            table_step(i)
 
         def quantize_x(j):
             nc.vector.quantize_mx(out=x_codes[j][:].bitcast(FP8X4), scales=x_scales[j][:], in_=x_grouped[j][:])
@@ -141,8 +150,6 @@ def tile_wqkv_pa_kernel(tc, Q_in, W_Q_bytes, W_Q_scale, W_K, out_0, out_1):
                 nc.scalar.activation(out=wq_w[g][:, t, cols], in_=src, func=ACT.Copy, scale=sc[:, g, t:t + 1])
             else:
                 nc.vector.tensor_scalar(out=wq_w[g][:, t, cols], in0=src, scalar1=sc[:, g, t:t + 1], scalar2=None, op0=ALU.mult)
-            if plane in WARM_PLANES:
-                keep_warm(wq_w[g][:, t, cols])
 
         def interleave(u, g):
             kind, h = u
@@ -189,19 +196,27 @@ def tile_wqkv_pa_kernel(tc, Q_in, W_Q_bytes, W_Q_scale, W_K, out_0, out_1):
             else:
                 nc.scalar.copy(out=stage[u][:, i, :], in_=acc[:])
 
-        for plane in V_HEAD:
-            widen(plane, False)
-        for plane in S_HEAD:
-            widen(plane, True)
+        for t in range(3):
+            widen((0, 1, t), False)
+        widen((0, 1, 3), True)
+        widen((0, 0, 0), True)
+        widen((0, 0, 1), True)
         interleave(Q1, 0)
-        interleave(Q1, 1)
         with tc.psum_pool(name="psum_x", bufs=2) as psum_x:
             turn_x(psum_x, 0)
             turn_x(psum_x, 1)
-            quantize_x(0)
+            widen((1, 1, 3), True)
+            widen((1, 1, 0), False)
             quantize(Q1, 0)
+            widen((1, 1, 1), False)
+            widen((1, 1, 2), False)
+            turn_x(psum_x, 2)
+            turn_x(psum_x, 3)
+            interleave(Q1, 1)
+            quantize_x(0)
             quantize(Q1, 1)
-            for j in range(1, NT // 2):
+            quantize_x(1)
+            for j in range(2, NT // 2):
                 turn_x(psum_x, 2 * j)
                 turn_x(psum_x, 2 * j + 1)
                 if j == NT // 2 - 1:

@@ -25,9 +25,7 @@ NJ = R // 2
 TWO_PI_HI = 6.28125
 TWO_PI_LO = 2.0 * math.pi - 6.28125
 
-Q1, K1, K0, Q0 = ("q", 1), ("k", 1), ("k", 0), ("q", 0)
-V_MID = ((0, 0, 2), (0, 0, 3), (1, 0, 0), (1, 0, 1), (1, 0, 2), (1, 0, 3))
-V_LAST = (1, 5)
+Q0, K0, K1, Q1 = ("q", 0), ("k", 0), ("k", 1), ("q", 1)
 WARM_START = 5
 
 
@@ -85,36 +83,36 @@ def tile_wqkv_pa_kernel(tc, Q_in, W_Q_bytes, W_Q_scale, W_K, out_0, out_1):
         make_identity(nc, ident[:])
 
         def table_tile(name, dtype=F32):
-            return [keep.tile([P, NT, NJ], dtype, name="%s%d" % (name, s)) for s in range(2)]
+            return keep.tile([P, 2, NT, NJ], dtype, name=name)
 
         z0 = table_tile("z0")
-        nc.vector.tensor_copy(out=z0[1][:, :, 0], in_=pos_i[:])
+        nc.vector.tensor_copy(out=z0[:, 1, :, 0], in_=pos_i[:])
         for n in (1, 2, 4):
-            nc.vector.tensor_scalar(out=z0[1][:, :, n:2 * n], in0=z0[1][:, :, 0:n], scalar1=10000.0 ** (-n / float(NJ)),
+            nc.vector.tensor_scalar(out=z0[:, 1, :, n:2 * n], in0=z0[:, 1, :, 0:n], scalar1=10000.0 ** (-n / float(NJ)),
                                     scalar2=None, op0=ALU.mult)
-        nc.vector.tensor_scalar(out=z0[0][:], in0=z0[1][:], scalar1=-0.5 * math.pi, scalar2=None, op0=ALU.add)
+        nc.vector.tensor_scalar(out=z0[:, 0], in0=z0[:, 1], scalar1=-0.5 * math.pi, scalar2=None, op0=ALU.add)
         turns = table_tile("turns", I32)
         z1, z2, y1, y2 = [table_tile(n) for n in ("z1", "z2", "y1", "y2")]
         for s in (1, 0):
-            nc.vector.tensor_scalar(out=turns[s][:], in0=z0[s][:], scalar1=1.0 / (2.0 * math.pi), scalar2=None, op0=ALU.mult)
+            nc.vector.tensor_scalar(out=turns[:, s], in0=z0[:, s], scalar1=1.0 / (2.0 * math.pi), scalar2=None, op0=ALU.mult)
         for s in (1, 0):
-            nc.vector.scalar_tensor_tensor(out=z1[s][:], in0=turns[s][:], scalar=-TWO_PI_HI, in1=z0[s][:], op0=ALU.mult, op1=ALU.add)
+            nc.vector.scalar_tensor_tensor(out=z1[:, s], in0=turns[:, s], scalar=-TWO_PI_HI, in1=z0[:, s], op0=ALU.mult, op1=ALU.add)
         for s in (1, 0):
-            nc.vector.scalar_tensor_tensor(out=z2[s][:], in0=turns[s][:], scalar=-TWO_PI_LO, in1=z1[s][:], op0=ALU.mult, op1=ALU.add)
-        cos_t = keep.tile([P, NT, R], F32, name="cos_t")
-        sin_t = keep.tile([P, NT, R], F32, name="sin_t")
+            nc.vector.scalar_tensor_tensor(out=z2[:, s], in0=turns[:, s], scalar=-TWO_PI_LO, in1=z1[:, s], op0=ALU.mult, op1=ALU.add)
+        cos_t = keep.tile([P, 2, NT, NJ], F32, name="cos_t")
+        sin_t = keep.tile([P, 2, NT, NJ], F32, name="sin_t")
 
         def table_step(n):
-            if n < 2:
-                nc.scalar.activation(out=y1[1 - n][:], in_=z2[1 - n][:], func=ACT.Abs)
+            if n == 0:
+                nc.scalar.activation(out=y1[:], in_=z2[:], func=ACT.Abs)
+            elif n == 1:
+                nc.scalar.activation(out=y2[:], in_=y1[:], func=ACT.Abs, bias=-math.pi)
             elif n < 4:
-                nc.scalar.activation(out=y2[3 - n][:], in_=y1[3 - n][:], func=ACT.Abs, bias=-math.pi)
-            elif n < 6:
-                nc.scalar.activation(out=cos_t[:, :, n - 4:R:2], in_=y2[1][:], func=ACT.Sin, bias=-0.5 * math.pi)
-            elif n == 6:
-                nc.scalar.activation(out=sin_t[:, :, 0:R:2], in_=y2[0][:], func=ACT.Sin, scale=-1.0, bias=0.5 * math.pi)
-            else:
-                nc.scalar.activation(out=sin_t[:, :, 1:R:2], in_=y2[0][:], func=ACT.Sin, bias=-0.5 * math.pi)
+                nc.scalar.activation(out=cos_t[:, n - 2], in_=y2[:, 1], func=ACT.Sin, bias=-0.5 * math.pi)
+            elif n == 4:
+                nc.scalar.activation(out=sin_t[:, 0], in_=y2[:, 0], func=ACT.Sin, scale=-1.0, bias=0.5 * math.pi)
+            elif n == 5:
+                nc.scalar.activation(out=sin_t[:, 1], in_=y2[:, 0], func=ACT.Sin, bias=-0.5 * math.pi)
 
         x_grouped = [keep.tile([P, 2048], BF16, name="x_grouped%d" % j, align_bytes=64) for j in range(NT // 2)]
         x_codes = [keep.tile([P, 512], U32, name="x_codes%d" % j, align_bytes=64) for j in range(NT // 2)]
@@ -135,7 +133,7 @@ def tile_wqkv_pa_kernel(tc, Q_in, W_Q_bytes, W_Q_scale, W_K, out_0, out_1):
         def quantize_x(j):
             nc.vector.quantize_mx(out=x_codes[j][:].bitcast(FP8X4), scales=x_scales[j][:], in_=x_grouped[j][:])
 
-        units = (Q1, K1, K0, Q0)
+        units = (Q0, K0, K1, Q1)
         wq_w = [keep.tile([P, 4, 1024], BF16, name="wq_w%d" % g) for g in range(NG)]
         w_grouped = {u: [keep.tile([P, NW, 4], BF16, name="w_grouped_%s%d_%d" % (u[0], u[1], g), align_bytes=64) for g in range(NG)] for u in units}
         w_codes = {u: [keep.tile([P, NW], U32, name="w_codes_%s%d_%d" % (u[0], u[1], g), align_bytes=64) for g in range(NG)] for u in units}
@@ -167,21 +165,26 @@ def tile_wqkv_pa_kernel(tc, Q_in, W_Q_bytes, W_Q_scale, W_K, out_0, out_1):
             quantize(u, 0)
             quantize(u, 1)
 
-        def rope_products(u, i0, i1):
-            x = stage[u]
-            t1 = keep.tile([P, i1 - i0, R], F32, name="t1_%s_%d" % (u[0], i0))
-            t2 = keep.tile([P, i1 - i0, R], F32, name="t2_%s_%d" % (u[0], i0))
-            nc.vector.tensor_tensor(out=t1[:], in0=x[:, i0:i1, 0:R], in1=cos_t[:, i0:i1, :], op=ALU.mult)
-            nc.vector.tensor_tensor(out=t2[:, :, 0:R:2], in0=x[:, i0:i1, 1:R:2], in1=sin_t[:, i0:i1, 0:R:2], op=ALU.mult)
-            nc.vector.tensor_tensor(out=t2[:, :, 1:R:2], in0=x[:, i0:i1, 0:R:2], in1=sin_t[:, i0:i1, 1:R:2], op=ALU.mult)
-            return t1, t2
+        def rope(u):
+            x = stage[u][:, :, 0:R].rearrange("p i (j e) -> p e i j", e=2)
+            t1 = keep.tile([P, 2, NT, NJ], F32, name="t1_%s" % u[0])
+            t2 = keep.tile([P, 2, NT, NJ], F32, name="t2_%s" % u[0])
+            y = keep.tile([P, NT, R], F32, name="y_%s" % u[0])
+            nc.vector.tensor_tensor(out=t2[:, 0], in0=x[:, 1], in1=sin_t[:, 0], op=ALU.mult)
+            nc.vector.tensor_tensor(out=t2[:, 1], in0=x[:, 0], in1=sin_t[:, 1], op=ALU.mult)
+            nc.vector.tensor_tensor(out=t1[:], in0=x, in1=cos_t[:], op=ALU.mult)
+            return t1, t2, y
 
-        def rope_sum(u, i0, i1, parts):
-            nc.vector.tensor_tensor(out=stage[u][:, i0:i1, 0:R], in0=parts[0][:], in1=parts[1][:], op=ALU.add)
+        def rope_sum(parts):
+            nc.vector.tensor_tensor(out=parts[2][:].rearrange("p i (j e) -> p e i j", e=2), in0=parts[0][:], in1=parts[1][:], op=ALU.add)
+
+        def store_rope(u, parts):
+            nc.sync.dma_start(out=out_views[u[0]][:, :, 0:R], in_=parts[2][:])
 
         def store(u, i0, i1):
             kind, h = u
-            nc.sync.dma_start(out=out_views[kind][:, i0:i1, h * NW:(h + 1) * NW], in_=stage[u][:, i0:i1, :])
+            c0 = R if h == 0 else 0
+            nc.sync.dma_start(out=out_views[kind][:, i0:i1, h * NW + c0:(h + 1) * NW], in_=stage[u][:, i0:i1, c0:NW])
 
         def one_pass(u, i, g, acc):
             j, ii = divmod(i, 2)
@@ -197,31 +200,33 @@ def tile_wqkv_pa_kernel(tc, Q_in, W_Q_bytes, W_Q_scale, W_K, out_0, out_1):
                 nc.scalar.copy(out=stage[u][:, i, :], in_=acc[:])
 
         for t in range(3):
-            widen((0, 1, t), False)
-        widen((0, 1, 3), True)
-        widen((0, 0, 0), True)
-        widen((0, 0, 1), True)
-        interleave(Q1, 0)
+            widen((0, 0, t), False)
+        widen((0, 0, 3), True)
+        widen((0, 1, 0), True)
+        widen((0, 1, 1), True)
+        widen((0, 1, 2), False)
+        interleave(Q0, 0)
+        widen((0, 1, 3), False)
+        quantize(Q0, 0)
         with tc.psum_pool(name="psum_x", bufs=2) as psum_x:
             turn_x(psum_x, 0)
             turn_x(psum_x, 1)
-            widen((1, 1, 3), True)
-            widen((1, 1, 0), False)
-            quantize(Q1, 0)
-            widen((1, 1, 1), False)
-            widen((1, 1, 2), False)
+            widen((1, 0, 3), True)
+            for t in range(3):
+                widen((1, 0, t), False)
+            quantize_x(0)
             turn_x(psum_x, 2)
             turn_x(psum_x, 3)
-            interleave(Q1, 1)
-            quantize_x(0)
-            quantize(Q1, 1)
+            interleave(Q0, 1)
             quantize_x(1)
-            for j in range(2, NT // 2):
-                turn_x(psum_x, 2 * j)
-                turn_x(psum_x, 2 * j + 1)
-                if j == NT // 2 - 1:
-                    interleave(K1, 0)
-                quantize_x(j)
+            quantize(Q0, 1)
+            turn_x(psum_x, 4)
+            turn_x(psum_x, 5)
+            quantize_x(2)
+            interleave(K0, 0)
+            turn_x(psum_x, 6)
+            turn_x(psum_x, 7)
+            quantize_x(3)
         psum_b = ctx.enter_context(tc.psum_pool(name="psum_b", bufs=2))
 
         def bank(i):
@@ -238,33 +243,40 @@ def tile_wqkv_pa_kernel(tc, Q_in, W_Q_bytes, W_Q_scale, W_K, out_0, out_1):
                 one_pass(u, i, 1, acc)
                 empty(u, i, acc, False)
 
-        interleave(K1, 1)
-        quantize(K1, 0)
-        quantize(K1, 1)
+        interleave(K0, 1)
+        quantize(K0, 0)
+        quantize(K0, 1)
+        for i in range(2):
+            tiles(Q0, i, i + 1)
+            store(Q0, i, i + 1)
+        for i in range(2, NT, 2):
+            tiles(Q0, i, i + 2)
+            store(Q0, i, i + 2)
+        prep_w(K1)
         for i in range(0, NT, 2):
-            tiles(Q1, i, i + 2)
-            store(Q1, i, i + 2)
-        prep_w(K0)
+            tiles(K0, i, i + 2)
+            store(K0, i, i + 2)
+        for t in range(0, 4):
+            widen((1, 1, t), False)
+        interleave(Q1, 0)
+        interleave(Q1, 1)
+        quantize(Q1, 0)
+        quantize(Q1, 1)
+        parts_q = rope(Q0)
+        parts_k = rope(K0)
+        rope_sum(parts_q)
+        rope_sum(parts_k)
         for i in range(0, NT, 2):
             tiles(K1, i, i + 2)
             store(K1, i, i + 2)
-        for plane in V_MID:
-            widen(plane, False)
-        for g in range(NG):
-            i0 = 4 * g
-            interleave(Q0, g)
-            tiles(K0, i0, i0 + 4)
-            parts = rope_products(K0, i0, i0 + 4)
-            quantize(Q0, g)
-            rope_sum(K0, i0, i0 + 4, parts)
-            store(K0, i0, i0 + 4)
-        banks = [bank(i) for i in range(NT)]
+        store_rope(Q0, parts_q)
+        store_rope(K0, parts_k)
         for i in range(NT):
-            one_pass(Q0, i, 0, banks[i])
-        for i in range(NT):
-            one_pass(Q0, i, 1, banks[i])
-            empty(Q0, i, banks[i], i in V_LAST)
-            if i % 2 == 1:
-                parts = rope_products(Q0, i - 1, i + 1)
-                rope_sum(Q0, i - 1, i + 1, parts)
-                store(Q0, i - 1, i + 1)
+            acc = bank(i)
+            one_pass(Q1, i, 0, acc)
+            one_pass(Q1, i, 1, acc)
+            empty(Q1, i, acc, i % 2 == 1)
+            if i in (1, 3, 5):
+                store(Q1, i - 1, i + 1)
+            if i > 5:
+                store(Q1, i, i + 1)

@@ -183,8 +183,7 @@ def tile_wqkv_pa_kernel(tc, Q_in, W_Q_bytes, W_Q_scale, W_K, out_0, out_1):
 
         def store(u, i0, i1):
             kind, h = u
-            c0 = R if h == 0 else 0
-            nc.sync.dma_start(out=out_views[kind][:, i0:i1, h * NW + c0:(h + 1) * NW], in_=stage[u][:, i0:i1, c0:NW])
+            nc.sync.dma_start(out=out_views[kind][:, i0:i1, h * NW:(h + 1) * NW], in_=stage[u][:, i0:i1, :])
 
         def one_pass(u, i, g, acc):
             j, ii = divmod(i, 2)

@@ -133,7 +133,7 @@ def tile_wqkv_pa_kernel(tc, Q_in, W_Q_bytes, W_Q_scale, W_K, out_0, out_1):
         def quantize_x(j):
             nc.vector.quantize_mx(out=x_codes[j][:].bitcast(FP8X4), scales=x_scales[j][:], in_=x_grouped[j][:])
 
-        units = (Q0, K0, K1, Q1)
+        units = (Q1, K1, K0, Q0)
         wq_w = [keep.tile([P, 4, 1024], BF16, name="wq_w%d" % g) for g in range(NG)]
         w_grouped = {u: [keep.tile([P, NW, 4], BF16, name="w_grouped_%s%d_%d" % (u[0], u[1], g), align_bytes=64) for g in range(NG)] for u in units}
         w_codes = {u: [keep.tile([P, NW], U32, name="w_codes_%s%d_%d" % (u[0], u[1], g), align_bytes=64) for g in range(NG)] for u in units}
@@ -165,21 +165,17 @@ def tile_wqkv_pa_kernel(tc, Q_in, W_Q_bytes, W_Q_scale, W_K, out_0, out_1):
             quantize(u, 0)
             quantize(u, 1)
 
-        def rope(u):
-            x = stage[u][:, :, 0:R].rearrange("p i (j e) -> p e i j", e=2)
-            t1 = keep.tile([P, 2, NT, NJ], F32, name="t1_%s" % u[0])
-            t2 = keep.tile([P, 2, NT, NJ], F32, name="t2_%s" % u[0])
-            y = keep.tile([P, NT, R], F32, name="y_%s" % u[0])
-            nc.vector.tensor_tensor(out=t2[:, 0], in0=x[:, 1], in1=sin_t[:, 0], op=ALU.mult)
-            nc.vector.tensor_tensor(out=t2[:, 1], in0=x[:, 0], in1=sin_t[:, 1], op=ALU.mult)
-            nc.vector.tensor_tensor(out=t1[:], in0=x, in1=cos_t[:], op=ALU.mult)
-            return t1, t2, y
+        def rope_products(u, i0, i1):
+            x = stage[u][:, i0:i1, 0:R].rearrange("p i (j e) -> p e i j", e=2)
+            t1 = keep.tile([P, 2, i1 - i0, NJ], F32, name="t1_%s_%d" % (u[0], i0))
+            t2 = keep.tile([P, 2, i1 - i0, NJ], F32, name="t2_%s_%d" % (u[0], i0))
+            nc.vector.tensor_tensor(out=t2[:, 0], in0=x[:, 1], in1=sin_t[:, 0, i0:i1], op=ALU.mult)
+            nc.vector.tensor_tensor(out=t2[:, 1], in0=x[:, 0], in1=sin_t[:, 1, i0:i1], op=ALU.mult)
+            nc.vector.tensor_tensor(out=t1[:], in0=x, in1=cos_t[:, :, i0:i1], op=ALU.mult)
+            return t1, t2
 
-        def rope_sum(parts):
-            nc.vector.tensor_tensor(out=parts[2][:].rearrange("p i (j e) -> p e i j", e=2), in0=parts[0][:], in1=parts[1][:], op=ALU.add)
-
-        def store_rope(u, parts):
-            nc.sync.dma_start(out=out_views[u[0]][:, :, 0:R], in_=parts[2][:])
+        def rope_sum(u, i0, i1, parts):
+            nc.vector.tensor_tensor(out=stage[u][:, i0:i1, 0:R].rearrange("p i (j e) -> p e i j", e=2), in0=parts[0][:], in1=parts[1][:], op=ALU.add)
 
         def store(u, i0, i1):
             kind, h = u
@@ -199,30 +195,30 @@ def tile_wqkv_pa_kernel(tc, Q_in, W_Q_bytes, W_Q_scale, W_K, out_0, out_1):
                 nc.scalar.copy(out=stage[u][:, i, :], in_=acc[:])
 
         for t in range(3):
-            widen((0, 0, t), False)
-        widen((0, 0, 3), True)
-        widen((0, 1, 0), True)
-        widen((0, 1, 1), True)
-        widen((0, 1, 2), False)
-        interleave(Q0, 0)
-        widen((0, 1, 3), False)
-        quantize(Q0, 0)
+            widen((0, 1, t), False)
+        widen((0, 1, 3), True)
+        widen((0, 0, 0), True)
+        widen((0, 0, 1), True)
+        widen((0, 0, 2), False)
+        interleave(Q1, 0)
+        widen((0, 0, 3), False)
+        quantize(Q1, 0)
         with tc.psum_pool(name="psum_x", bufs=2) as psum_x:
             turn_x(psum_x, 0)
             turn_x(psum_x, 1)
-            widen((1, 0, 3), True)
+            widen((1, 1, 3), True)
             for t in range(3):
-                widen((1, 0, t), False)
+                widen((1, 1, t), False)
             quantize_x(0)
             turn_x(psum_x, 2)
             turn_x(psum_x, 3)
-            interleave(Q0, 1)
+            interleave(Q1, 1)
             quantize_x(1)
-            quantize(Q0, 1)
+            quantize(Q1, 1)
             turn_x(psum_x, 4)
             turn_x(psum_x, 5)
             quantize_x(2)
-            interleave(K0, 0)
+            interleave(K1, 0)
             turn_x(psum_x, 6)
             turn_x(psum_x, 7)
             quantize_x(3)
@@ -235,47 +231,51 @@ def tile_wqkv_pa_kernel(tc, Q_in, W_Q_bytes, W_Q_scale, W_K, out_0, out_1):
                 acc = psum_b.tile([P, NW], F32, name="acc_b")
             return acc
 
-        def tiles(u, i0, i1):
+        def tiles(u, i0, i1, on_vector=()):
             for i in range(i0, i1):
                 acc = bank(i)
                 one_pass(u, i, 0, acc)
                 one_pass(u, i, 1, acc)
-                empty(u, i, acc, False)
+                empty(u, i, acc, i in on_vector)
 
-        interleave(K0, 1)
-        quantize(K0, 0)
-        quantize(K0, 1)
+        interleave(K1, 1)
+        quantize(K1, 0)
+        quantize(K1, 1)
         for i in range(2):
-            tiles(Q0, i, i + 1)
-            store(Q0, i, i + 1)
+            tiles(Q1, i, i + 1)
+            store(Q1, i, i + 1)
         for i in range(2, NT, 2):
-            tiles(Q0, i, i + 2)
-            store(Q0, i, i + 2)
-        prep_w(K1)
-        for i in range(0, NT, 2):
-            tiles(K0, i, i + 2)
-            store(K0, i, i + 2)
-        for t in range(0, 4):
-            widen((1, 1, t), False)
-        interleave(Q1, 0)
-        interleave(Q1, 1)
-        quantize(Q1, 0)
-        quantize(Q1, 1)
-        parts_q = rope(Q0)
-        parts_k = rope(K0)
-        rope_sum(parts_q)
-        rope_sum(parts_k)
+            tiles(Q1, i, i + 2)
+            store(Q1, i, i + 2)
+        prep_w(K0)
         for i in range(0, NT, 2):
             tiles(K1, i, i + 2)
             store(K1, i, i + 2)
-        store_rope(Q0, parts_q)
-        store_rope(K0, parts_k)
+        for t in range(0, 4):
+            widen((1, 0, t), False)
+        interleave(Q0, 0)
+        tiles(K0, 0, 2)
+        parts = rope_products(K0, 0, 2)
+        quantize(Q0, 0)
+        rope_sum(K0, 0, 2, parts)
+        store(K0, 0, 2)
+        tiles(K0, 2, 4)
+        parts = rope_products(K0, 2, 4)
+        tiles(K0, 4, 8)
+        interleave(Q0, 1)
+        rope_sum(K0, 2, 4, parts)
+        store(K0, 2, 4)
+        parts = rope_products(K0, 4, 8)
+        quantize(Q0, 1)
+        rope_sum(K0, 4, 8, parts)
+        store(K0, 4, 8)
+        banks = [bank(i) for i in range(NT)]
         for i in range(NT):
-            acc = bank(i)
-            one_pass(Q1, i, 0, acc)
-            one_pass(Q1, i, 1, acc)
-            empty(Q1, i, acc, i % 2 == 1)
-            if i in (1, 3, 5):
-                store(Q1, i - 1, i + 1)
-            if i > 5:
-                store(Q1, i, i + 1)
+            one_pass(Q0, i, 0, banks[i])
+        for i in range(NT):
+            one_pass(Q0, i, 1, banks[i])
+            empty(Q0, i, banks[i], i in (1, 5))
+            if i % 2 == 1:
+                parts = rope_products(Q0, i - 1, i + 1)
+                rope_sum(Q0, i - 1, i + 1, parts)
+                store(Q0, i - 1, i + 1)

@@ -254,28 +254,19 @@ def tile_wqkv_pa_kernel(tc, Q_in, W_Q_bytes, W_Q_scale, W_K, out_0, out_1):
         for t in range(0, 4):
             widen((1, 0, t), False)
         interleave(Q0, 0)
-        tiles(K0, 0, 2)
-        parts = rope_products(K0, 0, 2)
-        quantize(Q0, 0)
-        rope_sum(K0, 0, 2, parts)
-        store(K0, 0, 2)
-        tiles(K0, 2, 4)
-        parts = rope_products(K0, 2, 4)
-        tiles(K0, 4, 8)
         interleave(Q0, 1)
-        rope_sum(K0, 2, 4, parts)
-        store(K0, 2, 4)
-        parts = rope_products(K0, 4, 8)
+        tiles(K0, 0, 4)
+        parts = rope_products(K0, 0, 4)
+        rope_sum(K0, 0, 4, parts)
+        store(K0, 0, 4)
+        quantize(Q0, 0)
         quantize(Q0, 1)
+        tiles(K0, 4, 8)
+        parts = rope_products(K0, 4, 8)
         rope_sum(K0, 4, 8, parts)
         store(K0, 4, 8)
-        banks = [bank(i) for i in range(NT)]
-        for i in range(NT):
-            one_pass(Q0, i, 0, banks[i])
-        for i in range(NT):
-            one_pass(Q0, i, 1, banks[i])
-            empty(Q0, i, banks[i], i in (1, 5))
-            if i % 2 == 1:
-                parts = rope_products(Q0, i - 1, i + 1)
-                rope_sum(Q0, i - 1, i + 1, parts)
-                store(Q0, i - 1, i + 1)
+        for i0 in range(0, NT, 2):
+            tiles(Q0, i0, i0 + 2)
+            parts = rope_products(Q0, i0, i0 + 2)
+            rope_sum(Q0, i0, i0 + 2, parts)
+            store(Q0, i0, i0 + 2)

@@ -256,10 +256,10 @@ def tile_wqkv_pa_kernel(tc, Q_in, W_Q_bytes, W_Q_scale, W_K, out_0, out_1):
         interleave(Q0, 0)
         interleave(Q0, 1)
         tiles(K0, 0, 4)
+        quantize(Q0, 0)
         parts = rope_products(K0, 0, 4)
         rope_sum(K0, 0, 4, parts)
         store(K0, 0, 4)
-        quantize(Q0, 0)
         quantize(Q0, 1)
         tiles(K0, 4, 8)
         parts = rope_products(K0, 4, 8)

@@ -181,6 +181,14 @@ def tile_wqkv_pa_kernel(tc, Q_in, W_Q_bytes, W_Q_scale, W_K, out_0, out_1):
             kind, h = u
             nc.sync.dma_start(out=out_views[kind][:, i0:i1, h * NW:(h + 1) * NW], in_=stage[u][:, i0:i1, :])
 
+        def store_plain(u, i0, i1):
+            nc.sync.dma_start(out=out_views[u[0]][:, i0:i1, R:NW], in_=stage[u][:, i0:i1, R:NW])
+
+        def rope_sum_apart(u, i0, i1, parts):
+            y = keep.tile([P, i1 - i0, R], F32, name="y_%s_%d" % (u[0], i0))
+            nc.vector.tensor_tensor(out=y[:].rearrange("p i (j e) -> p e i j", e=2), in0=parts[0][:], in1=parts[1][:], op=ALU.add)
+            nc.sync.dma_start(out=out_views[u[0]][:, i0:i1, 0:R], in_=y[:])
+
         def one_pass(u, i, g, acc):
             j, ii = divmod(i, 2)
             cols = slice((ii * NG + g) * P, (ii * NG + g + 1) * P)
@@ -255,16 +263,20 @@ def tile_wqkv_pa_kernel(tc, Q_in, W_Q_bytes, W_Q_scale, W_K, out_0, out_1):
             widen((1, 0, t), False)
         interleave(Q0, 0)
         interleave(Q0, 1)
-        tiles(K0, 0, 4)
+        tiles(K0, 0, 2)
+        store_plain(K0, 0, 2)
+        tiles(K0, 2, 4)
+        store_plain(K0, 2, 4)
         quantize(Q0, 0)
         parts = rope_products(K0, 0, 4)
-        rope_sum(K0, 0, 4, parts)
-        store(K0, 0, 4)
+        rope_sum_apart(K0, 0, 4, parts)
         quantize(Q0, 1)
-        tiles(K0, 4, 8)
+        tiles(K0, 4, 6)
+        store_plain(K0, 4, 6)
+        tiles(K0, 6, 8)
+        store_plain(K0, 6, 8)
         parts = rope_products(K0, 4, 8)
-        rope_sum(K0, 4, 8, parts)
-        store(K0, 4, 8)
+        rope_sum_apart(K0, 4, 8, parts)
         for i0 in range(0, NT, 2):
             tiles(Q0, i0, i0 + 2)
             parts = rope_products(Q0, i0, i0 + 2)

@@ -27,13 +27,14 @@ TWO_PI_LO = 2.0 * math.pi - 6.28125
 
 Q0, K0, K1, Q1 = ("q", 0), ("k", 0), ("k", 1), ("q", 1)
 WARM_START = 5
+XB = 3
 
 
 def tile_wqkv_pa_kernel(tc, Q_in, W_Q_bytes, W_Q_scale, W_K, out_0, out_1):
     nc = tc.nc
     with ExitStack() as ctx:
         keep = ctx.enter_context(tc.tile_pool(name="keep", bufs=1))
-        psum_a = ctx.enter_context(tc.psum_pool(name="psum_a", bufs=6))
+        psum_a = ctx.enter_context(tc.psum_pool(name="psum_a", bufs=8 - XB))
         ctx.enter_context(tc.manual_schedule())
 
         x_view = Q_in.rearrange("o (p i) k -> p (o i) k", i=NT)
@@ -123,7 +124,8 @@ def tile_wqkv_pa_kernel(tc, Q_in, W_Q_bytes, W_Q_scale, W_K, out_0, out_1):
             grouped_words = x_grouped[j][:].bitcast(F32).rearrange("p (i g r u) -> p i g r u", i=2, g=NG, r=P, u=2)
             words = x_raw[j][:, ii, :].bitcast(F32)
             xt = pool.tile([P, NG, 2, P], F32, name="xt")
-            keep_warm(x_raw[j][:, ii, 0:NW])
+            if i > 0:
+                keep_warm(x_raw[j][:, ii, 0:NW])
             for g in range(NG):
                 for u in range(2):
                     nc.tensor.transpose(xt[:, g, u, :], words[:, 256 * g + u:256 * (g + 1):2], ident[:])
@@ -211,11 +213,12 @@ def tile_wqkv_pa_kernel(tc, Q_in, W_Q_bytes, W_Q_scale, W_K, out_0, out_1):
         interleave(Q1, 0)
         widen((0, 0, 3), False)
         quantize(Q1, 0)
-        with tc.psum_pool(name="psum_x", bufs=2) as psum_x:
+        with tc.psum_pool(name="psum_x", bufs=XB) as psum_x:
             turn_x(psum_x, 0)
             turn_x(psum_x, 1)
             widen((1, 1, 3), True)
-            for t in range(3):
+            widen((1, 1, 2), True)
+            for t in range(2):
                 widen((1, 1, t), False)
             quantize_x(0)
             turn_x(psum_x, 2)
@@ -230,10 +233,10 @@ def tile_wqkv_pa_kernel(tc, Q_in, W_Q_bytes, W_Q_scale, W_K, out_0, out_1):
             turn_x(psum_x, 6)
             turn_x(psum_x, 7)
             quantize_x(3)
-        psum_b = ctx.enter_context(tc.psum_pool(name="psum_b", bufs=2))
+        psum_b = ctx.enter_context(tc.psum_pool(name="psum_b", bufs=XB))
 
         def bank(i):
-            if i < 6:
+            if i < 8 - XB:
                 acc = psum_a.tile([P, NW], F32, name="acc_a")
             else:
                 acc = psum_b.tile([P, NW], F32, name="acc_b")
@@ -256,27 +259,27 @@ def tile_wqkv_pa_kernel(tc, Q_in, W_Q_bytes, W_Q_scale, W_K, out_0, out_1):
             tiles(Q1, i, i + 2)
             store(Q1, i, i + 2)
         prep_w(K0)
-        for i in range(0, NT, 2):
+        accs = [bank(i) for i in range(2)]
+        for i in range(2):
+            one_pass(K1, i, 0, accs[i])
+        for i in range(2):
+            one_pass(K1, i, 1, accs[i])
+            empty(K1, i, accs[i], False)
+        store(K1, 0, 2)
+        for i in range(2, NT, 2):
             tiles(K1, i, i + 2)
             store(K1, i, i + 2)
         for t in range(0, 4):
             widen((1, 0, t), False)
         interleave(Q0, 0)
         interleave(Q0, 1)
-        tiles(K0, 0, 2)
-        store_plain(K0, 0, 2)
-        tiles(K0, 2, 4)
-        store_plain(K0, 2, 4)
         quantize(Q0, 0)
-        parts = rope_products(K0, 0, 4)
-        rope_sum_apart(K0, 0, 4, parts)
         quantize(Q0, 1)
-        tiles(K0, 4, 6)
-        store_plain(K0, 4, 6)
-        tiles(K0, 6, 8)
-        store_plain(K0, 6, 8)
-        parts = rope_products(K0, 4, 8)
-        rope_sum_apart(K0, 4, 8, parts)
+        for i in range(0, NT, 2):
+            tiles(K0, i, i + 2)
+            store_plain(K0, i, i + 2)
+        parts = rope_products(K0, 0, NT)
+        rope_sum_apart(K0, 0, NT, parts)
         for i0 in range(0, NT, 2):
             tiles(Q0, i0, i0 + 2)
             parts = rope_products(Q0, i0, i0 + 2)

@@ -179,12 +179,12 @@ def tile_wqkv_pa_kernel(tc, Q_in, W_Q_bytes, W_Q_scale, W_K, out_0, out_1):
         def rope_sum(u, i0, i1, parts):
             nc.vector.tensor_tensor(out=stage[u][:, i0:i1, 0:R].rearrange("p i (j e) -> p e i j", e=2), in0=parts[0][:], in1=parts[1][:], op=ALU.add)
 
-        def store(u, i0, i1):
+        def store(u, i0, i1, queue=nc.sync):
             kind, h = u
-            nc.sync.dma_start(out=out_views[kind][:, i0:i1, h * NW:(h + 1) * NW], in_=stage[u][:, i0:i1, :])
+            queue.dma_start(out=out_views[kind][:, i0:i1, h * NW:(h + 1) * NW], in_=stage[u][:, i0:i1, :])
 
-        def store_plain(u, i0, i1):
-            nc.sync.dma_start(out=out_views[u[0]][:, i0:i1, R:NW], in_=stage[u][:, i0:i1, R:NW])
+        def store_plain(u, i0, i1, queue=nc.sync):
+            queue.dma_start(out=out_views[u[0]][:, i0:i1, R:NW], in_=stage[u][:, i0:i1, R:NW])
 
         def rope_sum_apart(u, i0, i1, parts):
             y = keep.tile([P, i1 - i0, R], F32, name="y_%s_%d" % (u[0], i0))
@@ -242,12 +242,26 @@ def tile_wqkv_pa_kernel(tc, Q_in, W_Q_bytes, W_Q_scale, W_K, out_0, out_1):
                 acc = psum_b.tile([P, NW], F32, name="acc_b")
             return acc
 
+        later = []
+
+        def flush():
+            while later:
+                fn, u, i0, i1 = later.pop()
+                fn(u, i0, i1, nc.scalar)
+
         def tiles(u, i0, i1, on_vector=()):
             for i in range(i0, i1):
                 acc = bank(i)
                 one_pass(u, i, 0, acc)
                 one_pass(u, i, 1, acc)
                 empty(u, i, acc, i in on_vector)
+                flush()
+
+        def store_pair(fn, u, i):
+            if i % 4 == 0:
+                fn(u, i, i + 2)
+            else:
+                later.append((fn, u, i, i + 2))
 
         interleave(K1, 1)
         quantize(K1, 0)
@@ -257,7 +271,7 @@ def tile_wqkv_pa_kernel(tc, Q_in, W_Q_bytes, W_Q_scale, W_K, out_0, out_1):
             store(Q1, i, i + 1)
         for i in range(2, NT, 2):
             tiles(Q1, i, i + 2)
-            store(Q1, i, i + 2)
+            store_pair(store, Q1, i)
         prep_w(K0)
         accs = [bank(i) for i in range(2)]
         for i in range(2):
@@ -265,10 +279,11 @@ def tile_wqkv_pa_kernel(tc, Q_in, W_Q_bytes, W_Q_scale, W_K, out_0, out_1):
         for i in range(2):
             one_pass(K1, i, 1, accs[i])
             empty(K1, i, accs[i], False)
-        store(K1, 0, 2)
+            flush()
+        store_pair(store, K1, 0)
         for i in range(2, NT, 2):
             tiles(K1, i, i + 2)
-            store(K1, i, i + 2)
+            store_pair(store, K1, i)
         for t in range(0, 4):
             widen((1, 0, t), False)
         interleave(Q0, 0)
@@ -277,11 +292,14 @@ def tile_wqkv_pa_kernel(tc, Q_in, W_Q_bytes, W_Q_scale, W_K, out_0, out_1):
         quantize(Q0, 1)
         for i in range(0, NT, 2):
             tiles(K0, i, i + 2)
-            store_plain(K0, i, i + 2)
+            store_pair(store_plain, K0, i)
         parts = rope_products(K0, 0, NT)
         rope_sum_apart(K0, 0, NT, parts)
         for i0 in range(0, NT, 2):
             tiles(Q0, i0, i0 + 2)
             parts = rope_products(Q0, i0, i0 + 2)
             rope_sum(Q0, i0, i0 + 2, parts)
-            store(Q0, i0, i0 + 2)
+            if i0 == 2:
+                later.append((store, Q0, i0, i0 + 2))
+            else:
+                store(Q0, i0, i0 + 2)

@@ -124,7 +124,7 @@ def tile_wqkv_pa_kernel(tc, Q_in, W_Q_bytes, W_Q_scale, W_K, out_0, out_1):
             grouped_words = x_grouped[j][:].bitcast(F32).rearrange("p (i g r u) -> p i g r u", i=2, g=NG, r=P, u=2)
             words = x_raw[j][:, ii, :].bitcast(F32)
             xt = pool.tile([P, NG, 2, P], F32, name="xt")
-            if i > 0:
+            if i in (1, 2, 3, 4, 6):
                 keep_warm(x_raw[j][:, ii, 0:NW])
             for g in range(NG):
                 for u in range(2):
@@ -136,7 +136,7 @@ def tile_wqkv_pa_kernel(tc, Q_in, W_Q_bytes, W_Q_scale, W_K, out_0, out_1):
             nc.vector.quantize_mx(out=x_codes[j][:].bitcast(FP8X4), scales=x_scales[j][:], in_=x_grouped[j][:])
 
         units = (Q1, K1, K0, Q0)
-        wq_w = [keep.tile([P, 4, 1024], BF16, name="wq_w%d" % g) for g in range(NG)]
+        wq_w = {(g, h): keep.tile([P, 4, NW], BF16, name="wq_w%d%d" % (g, h)) for g in range(NG) for h in range(2)}
         w_grouped = {u: [keep.tile([P, NW, 4], BF16, name="w_grouped_%s%d_%d" % (u[0], u[1], g), align_bytes=64) for g in range(NG)] for u in units}
         w_codes = {u: [keep.tile([P, NW], U32, name="w_codes_%s%d_%d" % (u[0], u[1], g), align_bytes=64) for g in range(NG)] for u in units}
         w_scales = {u: [keep.tile([P, NW], U8, name="w_scales_%s%d_%d" % (u[0], u[1], g), align_bytes=64) for g in range(NG)] for u in units}
@@ -144,18 +144,17 @@ def tile_wqkv_pa_kernel(tc, Q_in, W_Q_bytes, W_Q_scale, W_K, out_0, out_1):
 
         def widen(plane, on_scalar):
             g, h, t = plane
-            cols = slice(h * NW, (h + 1) * NW)
-            src = wq_b[g][:, t, cols].bitcast(FP8)
+            src = wq_b[g][:, t, h * NW:(h + 1) * NW].bitcast(FP8)
             if on_scalar:
-                nc.scalar.activation(out=wq_w[g][:, t, cols], in_=src, func=ACT.Copy, scale=sc[:, g, t:t + 1])
+                nc.scalar.activation(out=wq_w[g, h][:, t, :], in_=src, func=ACT.Copy, scale=sc[:, g, t:t + 1])
             else:
-                nc.vector.tensor_scalar(out=wq_w[g][:, t, cols], in0=src, scalar1=sc[:, g, t:t + 1], scalar2=None, op0=ALU.mult)
+                nc.vector.tensor_scalar(out=wq_w[g, h][:, t, :], in0=src, scalar1=sc[:, g, t:t + 1], scalar2=None, op0=ALU.mult)
 
         def interleave(u, g):
             kind, h = u
-            src = wq_w[g] if kind == "q" else wk_raw[g]
+            src = wq_w[g, h][:] if kind == "q" else wk_raw[g][:, :, h * NW:(h + 1) * NW]
             nc.vector.tensor_copy(out=w_grouped[u][g][:].rearrange("p (c i) t -> p c t i", i=4),
-                                  in_=src[:, :, h * NW:(h + 1) * NW].rearrange("p t (c i) -> p c t i", i=4))
+                                  in_=src.rearrange("p t (c i) -> p c t i", i=4))
 
         def quantize(u, g):
             nc.vector.quantize_mx(out=w_codes[u][g][:].bitcast(FP8X4), scales=w_scales[u][g][:],
@@ -224,8 +223,8 @@ def tile_wqkv_pa_kernel(tc, Q_in, W_Q_bytes, W_Q_scale, W_K, out_0, out_1):
             turn_x(psum_x, 2)
             turn_x(psum_x, 3)
             interleave(Q1, 1)
-            quantize_x(1)
             quantize(Q1, 1)
+            quantize_x(1)
             turn_x(psum_x, 4)
             turn_x(psum_x, 5)
             quantize_x(2)
@@ -257,21 +256,21 @@ def tile_wqkv_pa_kernel(tc, Q_in, W_Q_bytes, W_Q_scale, W_K, out_0, out_1):
                 empty(u, i, acc, i in on_vector)
                 flush()
 
-        def store_pair(fn, u, i):
-            if i % 4 == 0:
-                fn(u, i, i + 2)
-            else:
+        def store_pair(fn, u, i, phase):
+            if i % 4 == phase % 4:
                 later.append((fn, u, i, i + 2))
+            else:
+                fn(u, i, i + 2)
 
-        interleave(K1, 1)
         quantize(K1, 0)
+        interleave(K1, 1)
         quantize(K1, 1)
-        for i in range(2):
+        for i in range(4):
             tiles(Q1, i, i + 1)
             store(Q1, i, i + 1)
-        for i in range(2, NT, 2):
+        for i in range(4, NT, 2):
             tiles(Q1, i, i + 2)
-            store_pair(store, Q1, i)
+            store(Q1, i, i + 2)
         prep_w(K0)
         accs = [bank(i) for i in range(2)]
         for i in range(2):
@@ -280,10 +279,10 @@ def tile_wqkv_pa_kernel(tc, Q_in, W_Q_bytes, W_Q_scale, W_K, out_0, out_1):
             one_pass(K1, i, 1, accs[i])
             empty(K1, i, accs[i], False)
             flush()
-        store_pair(store, K1, 0)
+            store(K1, i, i + 1)
         for i in range(2, NT, 2):
             tiles(K1, i, i + 2)
-            store_pair(store, K1, i)
+            store_pair(store, K1, i, 4)
         for t in range(0, 4):
             widen((1, 0, t), False)
         interleave(Q0, 0)
@@ -292,14 +291,11 @@ def tile_wqkv_pa_kernel(tc, Q_in, W_Q_bytes, W_Q_scale, W_K, out_0, out_1):
         quantize(Q0, 1)
         for i in range(0, NT, 2):
             tiles(K0, i, i + 2)
-            store_pair(store_plain, K0, i)
+            store_pair(store_plain, K0, i, 0)
         parts = rope_products(K0, 0, NT)
         rope_sum_apart(K0, 0, NT, parts)
         for i0 in range(0, NT, 2):
             tiles(Q0, i0, i0 + 2)
             parts = rope_products(Q0, i0, i0 + 2)
             rope_sum(Q0, i0, i0 + 2, parts)
-            if i0 == 2:
-                later.append((store, Q0, i0, i0 + 2))
-            else:
-                store(Q0, i0, i0 + 2)
+            store(Q0, i0, i0 + 2, nc.scalar if i0 == NT - 2 else nc.sync)

@@ -124,7 +124,7 @@ def tile_wqkv_pa_kernel(tc, Q_in, W_Q_bytes, W_Q_scale, W_K, out_0, out_1):
             grouped_words = x_grouped[j][:].bitcast(F32).rearrange("p (i g r u) -> p i g r u", i=2, g=NG, r=P, u=2)
             words = x_raw[j][:, ii, :].bitcast(F32)
             xt = pool.tile([P, NG, 2, P], F32, name="xt")
-            if i in (1, 2, 3, 4, 6):
+            if i > 0:
                 keep_warm(x_raw[j][:, ii, 0:NW])
             for g in range(NG):
                 for u in range(2):

from contextlib import ExitStack
import math

import concourse.mybir as mybir
from concourse.masks import make_identity

FLOPS = 2 * 1024 * 1024 * 2048

F32 = mybir.dt.float32
BF16 = mybir.dt.bfloat16
U32 = mybir.dt.uint32
U8 = mybir.dt.uint8
I32 = mybir.dt.int32
FP8 = mybir.dt.float8_e4m3fn
FP8X4 = mybir.dt.float8_e4m3fn_x4
ALU = mybir.AluOpType
ACT = mybir.ActivationFunctionType

P = 128
NT = 8
NG = 2
NW = 512
R = 16
NJ = R // 2
TWO_PI_HI = 6.28125
TWO_PI_LO = 2.0 * math.pi - 6.28125

Q0, K0, K1, Q1 = ("q", 0), ("k", 0), ("k", 1), ("q", 1)
WARM_START = 5
XB = 3


def tile_wqkv_pa_kernel(tc, Q_in, W_Q_bytes, W_Q_scale, W_K, out_0, out_1):
    nc = tc.nc
    with ExitStack() as ctx:
        keep = ctx.enter_context(tc.tile_pool(name="keep", bufs=1))
        psum_a = ctx.enter_context(tc.psum_pool(name="psum_a", bufs=8 - XB))
        ctx.enter_context(tc.manual_schedule())

        x_view = Q_in.rearrange("o (p i) k -> p (o i) k", i=NT)
        wq_view = W_Q_bytes.rearrange("(g p t) n -> g p t n", p=P, t=4)
        wk_view = W_K.rearrange("(g p t) n -> g p t n", p=P, t=4)
        out_views = {
            "q": out_0.rearrange("o (p i) n -> p (o i) n", i=NT),
            "k": out_1.rearrange("o (p i) n -> p (o i) n", i=NT),
        }

        pos_i = keep.tile([P, NT], I32, name="pos_i")
        nc.gpsimd.iota(pos_i[:], pattern=[[1, NT]], base=0, channel_multiplier=NT)
        warm = keep.tile([P, NW], BF16, name="warm")
        nc.gpsimd.memset(warm[:], 0.0)
        idle_bank = psum_a.tile([P, NW], F32, name="acc_a")

        def keep_warm(rhs):
            nc.tensor.matmul(out=idle_bank[:], lhsT=warm[:, 0:P], rhs=rhs, start=True, stop=True)

        for n in range(WARM_START):
            keep_warm(warm[:])

        sc = keep.tile([P, NG, 4], F32, name="sc")
        nc.scalar.dma_start(out=sc[:], in_=W_Q_scale.rearrange("(g p t) o -> p g (t o)", p=P, t=4))
        preload = keep.tile([P, 1], F32, name="preload")
        nc.scalar.activation(out=preload[:], in_=warm[:, 0:1], func=ACT.Sin)
        wq_b = [keep.tile([P, 4, 1024], U8, name="wq_b%d" % g) for g in range(NG)]
        x_raw = [keep.tile([P, 2, 1024], BF16, name="x_raw%d" % j) for j in range(NT // 2)]
        wk_raw = [keep.tile([P, 4, 1024], BF16, name="wk_raw%d" % g) for g in range(NG)]

        def load_wq(g):
            nc.sync.dma_start(out=wq_b[g][:], in_=wq_view[g])

        def load_x(j):
            nc.sync.dma_start(out=x_raw[j][:], in_=x_view[:, 2 * j:2 * j + 2, :])

        load_wq(0)
        load_x(0)
        load_x(1)
        load_wq(1)
        load_x(2)
        load_x(3)
        for g in range(NG):
            nc.sync.dma_start(out=wk_raw[g][:], in_=wk_view[g])

        ident = keep.tile([P, P], F32, name="ident")
        make_identity(nc, ident[:])

        def table_tile(name, dtype=F32):
            return keep.tile([P, 2, NT, NJ], dtype, name=name)

        z0 = table_tile("z0")
        nc.vector.tensor_copy(out=z0[:, 1, :, 0], in_=pos_i[:])
        for n in (1, 2, 4):
            nc.vector.tensor_scalar(out=z0[:, 1, :, n:2 * n], in0=z0[:, 1, :, 0:n], scalar1=10000.0 ** (-n / float(NJ)),
                                    scalar2=None, op0=ALU.mult)
        nc.vector.tensor_scalar(out=z0[:, 0], in0=z0[:, 1], scalar1=-0.5 * math.pi, scalar2=None, op0=ALU.add)
        turns = table_tile("turns", I32)
        z1, z2, y1, y2 = [table_tile(n) for n in ("z1", "z2", "y1", "y2")]
        for s in (1, 0):
            nc.vector.tensor_scalar(out=turns[:, s], in0=z0[:, s], scalar1=1.0 / (2.0 * math.pi), scalar2=None, op0=ALU.mult)
        for s in (1, 0):
            nc.vector.scalar_tensor_tensor(out=z1[:, s], in0=turns[:, s], scalar=-TWO_PI_HI, in1=z0[:, s], op0=ALU.mult, op1=ALU.add)
        for s in (1, 0):
            nc.vector.scalar_tensor_tensor(out=z2[:, s], in0=turns[:, s], scalar=-TWO_PI_LO, in1=z1[:, s], op0=ALU.mult, op1=ALU.add)
        cos_t = keep.tile([P, 2, NT, NJ], F32, name="cos_t")
        sin_t = keep.tile([P, 2, NT, NJ], F32, name="sin_t")

        def table_step(n):
            if n == 0:
                nc.scalar.activation(out=y1[:], in_=z2[:], func=ACT.Abs)
            elif n == 1:
                nc.scalar.activation(out=y2[:], in_=y1[:], func=ACT.Abs, bias=-math.pi)
            elif n < 4:
                nc.scalar.activation(out=cos_t[:, n - 2], in_=y2[:, 1], func=ACT.Sin, bias=-0.5 * math.pi)
            elif n == 4:
                nc.scalar.activation(out=sin_t[:, 0], in_=y2[:, 0], func=ACT.Sin, scale=-1.0, bias=0.5 * math.pi)
            elif n == 5:
                nc.scalar.activation(out=sin_t[:, 1], in_=y2[:, 0], func=ACT.Sin, bias=-0.5 * math.pi)

        x_grouped = [keep.tile([P, 2048], BF16, name="x_grouped%d" % j, align_bytes=64) for j in range(NT // 2)]
        x_codes = [keep.tile([P, 512], U32, name="x_codes%d" % j, align_bytes=64) for j in range(NT // 2)]
        x_scales = [keep.tile([P, 512], U8, name="x_scales%d" % j, align_bytes=64) for j in range(NT // 2)]

        def turn_x(pool, i):
            j, ii = divmod(i, 2)
            grouped_words = x_grouped[j][:].bitcast(F32).rearrange("p (i g r u) -> p i g r u", i=2, g=NG, r=P, u=2)
            words = x_raw[j][:, ii, :].bitcast(F32)
            xt = pool.tile([P, NG, 2, P], F32, name="xt")
            if i > 0:
                keep_warm(x_raw[j][:, ii, 0:NW])
            for g in range(NG):
                for u in range(2):
                    nc.tensor.transpose(xt[:, g, u, :], words[:, 256 * g + u:256 * (g + 1):2], ident[:])
            nc.scalar.copy(out=grouped_words[:, ii], in_=xt[:].rearrange("p g u r -> p g r u"))
            table_step(i)

        def quantize_x(j):
            nc.vector.quantize_mx(out=x_codes[j][:].bitcast(FP8X4), scales=x_scales[j][:], in_=x_grouped[j][:])

        units = (Q1, K1, K0, Q0)
        wq_w = {(g, h): keep.tile([P, 4, NW], BF16, name="wq_w%d%d" % (g, h)) for g in range(NG) for h in range(2)}
        w_grouped = {u: [keep.tile([P, NW, 4], BF16, name="w_grouped_%s%d_%d" % (u[0], u[1], g), align_bytes=64) for g in range(NG)] for u in units}
        w_codes = {u: [keep.tile([P, NW], U32, name="w_codes_%s%d_%d" % (u[0], u[1], g), align_bytes=64) for g in range(NG)] for u in units}
        w_scales = {u: [keep.tile([P, NW], U8, name="w_scales_%s%d_%d" % (u[0], u[1], g), align_bytes=64) for g in range(NG)] for u in units}
        stage = {u: keep.tile([P, NT, NW], F32, name="stage_%s%d" % u) for u in units}

        def widen(plane, on_scalar):
            g, h, t = plane
            src = wq_b[g][:, t, h * NW:(h + 1) * NW].bitcast(FP8)
            if on_scalar:
                nc.scalar.activation(out=wq_w[g, h][:, t, :], in_=src, func=ACT.Copy, scale=sc[:, g, t:t + 1])
            else:
                nc.vector.tensor_scalar(out=wq_w[g, h][:, t, :], in0=src, scalar1=sc[:, g, t:t + 1], scalar2=None, op0=ALU.mult)

        def interleave(u, g):
            kind, h = u
            src = wq_w[g, h][:] if kind == "q" else wk_raw[g][:, :, h * NW:(h + 1) * NW]
            nc.vector.tensor_copy(out=w_grouped[u][g][:].rearrange("p (c i) t -> p c t i", i=4),
                                  in_=src.rearrange("p t (c i) -> p c t i", i=4))

        def quantize(u, g):
            nc.vector.quantize_mx(out=w_codes[u][g][:].bitcast(FP8X4), scales=w_scales[u][g][:],
                                  in_=w_grouped[u][g][:].rearrange("p c t -> p (c t)"))

        def prep_w(u):
            interleave(u, 0)
            interleave(u, 1)
            quantize(u, 0)
            quantize(u, 1)

        def rope_products(u, i0, i1):
            x = stage[u][:, i0:i1, 0:R].rearrange("p i (j e) -> p e i j", e=2)
            t1 = keep.tile([P, 2, i1 - i0, NJ], F32, name="t1_%s_%d" % (u[0], i0))
            t2 = keep.tile([P, 2, i1 - i0, NJ], F32, name="t2_%s_%d" % (u[0], i0))
            nc.vector.tensor_tensor(out=t2[:, 0], in0=x[:, 1], in1=sin_t[:, 0, i0:i1], op=ALU.mult)
            nc.vector.tensor_tensor(out=t2[:, 1], in0=x[:, 0], in1=sin_t[:, 1, i0:i1], op=ALU.mult)
            nc.vector.tensor_tensor(out=t1[:], in0=x, in1=cos_t[:, :, i0:i1], op=ALU.mult)
            return t1, t2

        def rope_sum(u, i0, i1, parts):
            nc.vector.tensor_tensor(out=stage[u][:, i0:i1, 0:R].rearrange("p i (j e) -> p e i j", e=2), in0=parts[0][:], in1=parts[1][:], op=ALU.add)

        def store(u, i0, i1, queue=nc.sync):
            kind, h = u
            queue.dma_start(out=out_views[kind][:, i0:i1, h * NW:(h + 1) * NW], in_=stage[u][:, i0:i1, :])

        def store_plain(u, i0, i1, queue=nc.sync):
            queue.dma_start(out=out_views[u[0]][:, i0:i1, R:NW], in_=stage[u][:, i0:i1, R:NW])

        def rope_sum_apart(u, i0, i1, parts):
            y = keep.tile([P, i1 - i0, R], F32, name="y_%s_%d" % (u[0], i0))
            nc.vector.tensor_tensor(out=y[:].rearrange("p i (j e) -> p e i j", e=2), in0=parts[0][:], in1=parts[1][:], op=ALU.add)
            nc.sync.dma_start(out=out_views[u[0]][:, i0:i1, 0:R], in_=y[:])

        def one_pass(u, i, g, acc):
            j, ii = divmod(i, 2)
            cols = slice((ii * NG + g) * P, (ii * NG + g + 1) * P)
            nc.tensor.matmul_mx(out=acc[:], lhsT=x_codes[j][:, cols].bitcast(FP8X4), lhsT_scale=x_scales[j][:, cols],
                                rhs=w_codes[u][g][:].bitcast(FP8X4), rhs_scale=w_scales[u][g][:],
                                start=(g == 0), stop=(g == NG - 1))

        def empty(u, i, acc, on_vector):
            if on_vector:
                nc.vector.tensor_copy(out=stage[u][:, i, :], in_=acc[:])
            else:
                nc.scalar.copy(out=stage[u][:, i, :], in_=acc[:])

        for t in range(3):
            widen((0, 1, t), False)
        widen((0, 1, 3), True)
        widen((0, 0, 0), True)
        widen((0, 0, 1), True)
        widen((0, 0, 2), False)
        interleave(Q1, 0)
        widen((0, 0, 3), False)
        quantize(Q1, 0)
        with tc.psum_pool(name="psum_x", bufs=XB) as psum_x:
            turn_x(psum_x, 0)
            turn_x(psum_x, 1)
            widen((1, 1, 3), True)
            widen((1, 1, 2), True)
            for t in range(2):
                widen((1, 1, t), False)
            quantize_x(0)
            turn_x(psum_x, 2)
            turn_x(psum_x, 3)
            interleave(Q1, 1)
            quantize(Q1, 1)
            quantize_x(1)
            turn_x(psum_x, 4)
            turn_x(psum_x, 5)
            quantize_x(2)
            interleave(K1, 0)
            turn_x(psum_x, 6)
            turn_x(psum_x, 7)
            quantize_x(3)
        psum_b = ctx.enter_context(tc.psum_pool(name="psum_b", bufs=XB))

        def bank(i):
            if i < 8 - XB:
                acc = psum_a.tile([P, NW], F32, name="acc_a")
            else:
                acc = psum_b.tile([P, NW], F32, name="acc_b")
            return acc

        later = []

        def flush():
            while later:
                fn, u, i0, i1 = later.pop()
                fn(u, i0, i1, nc.scalar)

        def tiles(u, i0, i1, on_vector=()):
            for i in range(i0, i1):
                acc = bank(i)
                one_pass(u, i, 0, acc)
                one_pass(u, i, 1, acc)
                empty(u, i, acc, i in on_vector)
                flush()

        def store_pair(fn, u, i, phase):
            if i % 4 == phase % 4:
                later.append((fn, u, i, i + 2))
            else:
                fn(u, i, i + 2)

        quantize(K1, 0)
        interleave(K1, 1)
        quantize(K1, 1)
        for i in range(4):
            tiles(Q1, i, i + 1)
            store(Q1, i, i + 1)
        for i in range(4, NT, 2):
            tiles(Q1, i, i + 2)
            store(Q1, i, i + 2)
        prep_w(K0)
        accs = [bank(i) for i in range(2)]
        for i in range(2):
            one_pass(K1, i, 0, accs[i])
        for i in range(2):
            one_pass(K1, i, 1, accs[i])
            empty(K1, i, accs[i], False)
            flush()
            store(K1, i, i + 1)
        for i in range(2, NT, 2):
            tiles(K1, i, i + 2)
            store_pair(store, K1, i, 4)
        for t in range(0, 4):
            widen((1, 0, t), False)
        interleave(Q0, 0)
        interleave(Q0, 1)
        quantize(Q0, 0)
        quantize(Q0, 1)
        for i in range(0, NT, 2):
            tiles(K0, i, i + 2)
            store_pair(store_plain, K0, i, 0)
        parts = rope_products(K0, 0, NT)
        rope_sum_apart(K0, 0, NT, parts)
        for i0 in range(0, NT, 2):
            tiles(Q0, i0, i0 + 2)
            parts = rope_products(Q0, i0, i0 + 2)
            rope_sum(Q0, i0, i0 + 2, parts)
            store(Q0, i0, i0 + 2, nc.scalar if i0 == NT - 2 else nc.sync)
